import numpy as np
import ml_dtypes


def mxq(x, axis, fmt="e4m3"):
    dtype, down = {"e4m3": (ml_dtypes.float8_e4m3fn, 7), "e5m2": (ml_dtypes.float8_e5m2, 14)}[fmt]
    v = np.moveaxis(np.asarray(x, np.float32).astype(ml_dtypes.bfloat16).astype(np.float64), axis, -1)
    blocks = v.reshape(v.shape[:-1] + (-1, 32))
    amax = np.abs(blocks).max(-1, keepdims=True)
    byte = np.maximum(np.where(amax > 0, np.frexp(amax)[1] - 1 + 127, 0) - down, 1)
    scale = np.exp2(byte - 127.0)
    codes = (blocks / scale).astype(np.float32).astype(dtype).astype(np.float64)
    return np.moveaxis((codes * scale).reshape(v.shape), -1, axis)


WIDE = False


def mx_kscale(k):
    if not WIDE:
        return np.ones(k)
    levels = np.array([10, -10, 5, -5, 0])
    a = np.random.permutation(np.resize(levels, k // 512 * 4)).reshape(k // 512, 4)
    idx = np.arange(k)
    return np.exp2(a[idx // 512, idx % 128 // 32])


BF16 = ml_dtypes.bfloat16


def bf(x):
    return np.asarray(x, np.float32).astype(BF16)


def f64(x):
    return np.asarray(x).astype(np.float64)


B, RES, C, NH, RD, RW = 4, 32, 512, 8, 16, 128
N, L = B * RES, RES
KG = L * RD


def setup_inputs():
    s = mx_kscale(C)
    return {"x_seq": bf(np.random.standard_normal((N, L, C)) * s),
            "Wc": bf(np.random.standard_normal((NH * RD, C)) / np.sqrt(C) / s),
            "bc": bf(np.random.standard_normal(NH * RD) * 0.3),
            "Wg": bf(np.random.standard_normal((L * L, KG)) * 1.5 / np.sqrt(KG)),
            "bg": bf(np.random.standard_normal(L * L) * 0.5)}


def reference(x_seq, Wc, bc, Wg, bg):
    w = (mxq(f64(x_seq), 2, "e4m3") @ mxq(f64(Wc), 1, "e4m3").T) + f64(bc)
    w = w.reshape(N, L, NH, RD).transpose(0, 2, 1, 3).reshape(N, NH, KG)
    w = ((mxq(w, 2, "e4m3") @ mxq(f64(Wg), 1, "e4m3").T) + f64(bg)).reshape(N, NH, L, L)
    e = np.exp(w - w.max(-2, keepdims=True))
    return e / e.sum(-2, keepdims=True)

@@ -1,0 +1,262 @@
+from contextlib import ExitStack
+
+import concourse.mybir as mybir
+from concourse.masks import make_identity
+
+F32 = mybir.dt.float32
+BF16 = mybir.dt.bfloat16
+U32 = mybir.dt.uint32
+U8 = mybir.dt.uint8
+FP8X4 = mybir.dt.float8_e4m3fn_x4
+ALU = mybir.AluOpType
+EXP = mybir.ActivationFunctionType.Exp
+
+P = 128
+PACK = 4
+BANK = 512
+
+SEQS, TOKENS, CHANNELS = 128, 32, 512
+HEADS, REDUCED = 8, 16
+MIX = TOKENS * TOKENS
+
+QUARTERS = PACK
+Q_TOKENS = TOKENS // QUARTERS
+GROUP_SEQS = P // QUARTERS
+GROUPS = SEQS // GROUP_SEQS
+ROW_TILES = GROUP_SEQS * HEADS // P
+ALL_ROW_TILES = GROUPS * ROW_TILES
+WORDS = CHANNELS // 2
+HALF_TOKENS = BANK // P
+HALVES = GROUPS * Q_TOKENS // HALF_TOKENS
+LEAD = 3
+
+FLOPS = 2 * SEQS * TOKENS * CHANNELS * HEADS * REDUCED + 2 * SEQS * HEADS * TOKENS * REDUCED * MIX
+
+
+def quantise(nc, codes, scales, grouped):
+    nc.vector.quantize_mx(out=codes.bitcast(FP8X4), scales=scales, in_=grouped)
+
+
+def mx_pass(nc, acc, lhsT, lhsT_scale, rhs, rhs_scale):
+    nc.tensor.matmul_mx(
+        out=acc,
+        lhsT=lhsT.bitcast(FP8X4),
+        lhsT_scale=lhsT_scale,
+        rhs=rhs.bitcast(FP8X4),
+        rhs_scale=rhs_scale,
+        start=True,
+        stop=True,
+    )
+
+
+def tile_dynamixerblock_pa_kernel(tc, x_seq, Wc, bc, Wg, bg, out):
+    nc = tc.nc
+    x_rows = x_seq.rearrange("n (a l) c -> (n a) (l c)", a=QUARTERS)
+    out_rows = out.rearrange("n h i j -> (n h) (i j)")
+
+    with ExitStack() as ctx:
+        const = ctx.enter_context(tc.tile_pool(name="const", bufs=1))
+        xin = ctx.enter_context(tc.tile_pool(name="xin", bufs=GROUPS))
+        work = ctx.enter_context(tc.tile_pool(name="work", bufs=2))
+        soft = ctx.enter_context(tc.tile_pool(name="soft", bufs=3))
+        psum = ctx.enter_context(tc.psum_pool(name="psum", bufs=1))
+        ctx.enter_context(tc.manual_schedule())
+
+        wc_sb = const.tile([P, CHANNELS], BF16)
+        nc.sync.dma_start(out=wc_sb[:], in_=Wc)
+        wg_sb = const.tile([P, MIX // P, TOKENS * REDUCED], BF16)
+        x_sb = []
+        half_row = HALF_TOKENS * CHANNELS
+        for g in range(GROUPS):
+            x_sb.append(xin.tile([P, Q_TOKENS * CHANNELS], BF16, name="x_sb"))
+            for part in range(2):
+                nc.sync.dma_start(
+                    out=x_sb[g][:, part * half_row : (part + 1) * half_row],
+                    in_=x_rows[g * P : (g + 1) * P, part * half_row : (part + 1) * half_row],
+                )
+            if g == 0:
+                nc.sync.dma_start(out=wg_sb[:], in_=Wg.rearrange("(s p) k -> p s k", p=P))
+        bc_all = const.tile([P, HEADS * REDUCED], BF16)
+        nc.scalar.dma_start(out=bc_all[:], in_=bc.partition_broadcast(P))
+        bg_all = const.tile([P, MIX], BF16)
+        nc.scalar.dma_start(out=bg_all[:], in_=bg.partition_broadcast(P))
+        bc_hlr = (
+            bc_all[:]
+            .rearrange("p (h r) -> p h r", h=HEADS)
+            .unsqueeze(2)
+            .to_broadcast([P, HEADS, HALF_TOKENS, REDUCED])
+        )
+
+        ident_f32 = const.tile([P, P], F32)
+        make_identity(nc, ident_f32[:])
+        ident_bf16 = const.tile([P, P], BF16)
+        make_identity(nc, ident_bf16[:])
+
+        wc_codes = const.tile([P, P], U32, align_bytes=64)
+        wc_scales = const.tile([P, P], U8, align_bytes=64)
+        wg_codes = const.tile([P, MIX], U32, align_bytes=64)
+        wg_scales = const.tile([P, MIX], U8, align_bytes=64)
+        bg_ji = const.tile([P, TOKENS, TOKENS], F32)
+
+        def prepare_wc():
+            wc_words = wc_sb[:].bitcast(F32)
+            wc_T = psum.tile([P, 2, P], F32, tag="xT", bufs=2)
+            for u in range(2):
+                nc.tensor.transpose(wc_T[:, u, :], wc_words[:, u * P : (u + 1) * P], ident_f32[:])
+            wc_grp = const.tile([P, P * PACK], BF16, align_bytes=64)
+            nc.vector.tensor_copy(
+                out=wc_grp[:].bitcast(F32).rearrange("p (m u) -> p m u", u=2),
+                in_=wc_T[:].rearrange("p u m -> p m u"),
+            )
+            quantise(nc, wc_codes[:], wc_scales[:], wc_grp[:])
+
+        def prepare_wg():
+            wg_grp = const.tile([P, MIX, PACK], BF16, align_bytes=64)
+            for pair in range(MIX // P // 2):
+                wg_T = psum.tile([P, 2, PACK, P], BF16, tag="xT", bufs=2)
+                for s in range(2):
+                    for t in range(PACK):
+                        nc.tensor.transpose(
+                            wg_T[:, s, t, :], wg_sb[:, 2 * pair + s, t * P : (t + 1) * P], ident_bf16[:]
+                        )
+                grouped = wg_grp[:, 2 * pair * P : (2 * pair + 2) * P, :].rearrange("p (s o) t -> p s o t", s=2)
+                if pair % 2 == 0:
+                    nc.scalar.copy(out=grouped, in_=wg_T[:].rearrange("p s t o -> p s o t"))
+                else:
+                    nc.vector.tensor_copy(out=grouped, in_=wg_T[:].rearrange("p s t o -> p s o t"))
+            quantise(nc, wg_codes[:], wg_scales[:], wg_grp[:].rearrange("p o t -> p (o t)"))
+
+        group_tiles = []
+
+        def channels_to_partitions(k):
+            g, part = divmod(k, 2)
+            if part == 0:
+                group_tiles.append(
+                    {
+                        "x_grp": work.tile([P, Q_TOKENS * P * PACK], BF16, align_bytes=64, name="x_grp"),
+                        "x_codes": work.tile([P, Q_TOKENS * P], U32, align_bytes=64, name="x_codes"),
+                        "x_scales": work.tile([P, Q_TOKENS * P], U8, align_bytes=64, name="x_scales"),
+                        "v_nat": work.tile([P, HEADS, Q_TOKENS, REDUCED], BF16, name="v_nat"),
+                        "v_codes": work.tile([P, GROUP_SEQS * HEADS], U32, align_bytes=64, name="v_codes"),
+                        "v_scales": work.tile([P, GROUP_SEQS * HEADS], U8, align_bytes=64, name="v_scales"),
+                    }
+                )
+            x_words = x_sb[g][:].bitcast(F32)
+            x_grp_words = group_tiles[g]["x_grp"][:].bitcast(F32).rearrange("p (l m u) -> p l m u", l=Q_TOKENS, u=2)
+            for pair in range(2 * part, 2 * part + 2):
+                x_T = psum.tile([P, 2, 2, P], F32, tag="xT", bufs=2)
+                for l2 in range(2):
+                    for u in range(2):
+                        first = (2 * pair + l2) * WORDS + u * P
+                        nc.tensor.transpose(x_T[:, l2, u, :], x_words[:, first : first + P], ident_f32[:])
+                nc.scalar.copy(out=x_grp_words[:, 2 * pair : 2 * pair + 2], in_=x_T[:].rearrange("p l u m -> p l m u"))
+
+        def quantise_x(k):
+            g, part = divmod(k, 2)
+            t = group_tiles[g]
+            cols = slice(part * BANK, (part + 1) * BANK)
+            quantise(
+                nc, t["x_codes"][:, cols], t["x_scales"][:, cols], t["x_grp"][:, part * BANK * PACK : (part + 1) * BANK * PACK]
+            )
+
+        def compress(k):
+            g, part = divmod(k, 2)
+            t = group_tiles[g]
+            u_ps = psum.tile([P, HALF_TOKENS, P], F32, tag="u", bufs=1)
+            for l4 in range(HALF_TOKENS):
+                m = slice((HALF_TOKENS * part + l4) * P, (HALF_TOKENS * part + l4 + 1) * P)
+                mx_pass(nc, u_ps[:, l4, :], t["x_codes"][:, m], t["x_scales"][:, m], wc_codes[:], wc_scales[:])
+            nc.vector.tensor_tensor(
+                out=t["v_nat"][:, :, HALF_TOKENS * part : HALF_TOKENS * (part + 1), :],
+                in0=u_ps[:].rearrange("p l (h r) -> p h l r", h=HEADS),
+                in1=bc_hlr,
+                op=ALU.add,
+            )
+
+        def flatten(g):
+            t = group_tiles[g]
+            v_T = psum.tile([P, GROUP_SEQS, HEADS, QUARTERS], BF16, tag="vT", bufs=1)
+            for h in range(HEADS):
+                nc.tensor.transpose(v_T[:, :, h, :], t["v_nat"][:, h, :, :].rearrange("p l r -> p (l r)"), ident_bf16[:])
+            v_grp = work.tile([P, GROUP_SEQS * HEADS * PACK], BF16, align_bytes=64)
+            nc.vector.tensor_copy(out=v_grp[:], in_=v_T[:].rearrange("p n h a -> p (n h a)"))
+            quantise(nc, t["v_codes"][:], t["v_scales"][:], v_grp[:])
+
+        row_tiles = []
+
+        def logits(rt):
+            g, part = divmod(rt, ROW_TILES)
+            t = group_tiles[g]
+            rows = slice(part * P, (part + 1) * P)
+            s_ji = soft.tile([P, TOKENS, TOKENS], F32)
+            i_bank = BANK // TOKENS
+            for b in range(MIX // BANK):
+                g_ps = psum.tile([P, BANK], F32, tag="g", bufs=4)
+                o_cols = slice(b * BANK, (b + 1) * BANK)
+                mx_pass(nc, g_ps[:], t["v_codes"][:, rows], t["v_scales"][:, rows], wg_codes[:, o_cols], wg_scales[:, o_cols])
+                nc.vector.tensor_tensor(
+                    out=s_ji[:, :, b * i_bank : (b + 1) * i_bank],
+                    in0=g_ps[:].rearrange("p (i j) -> p j i", j=TOKENS),
+                    in1=bg_ji[:, :, b * i_bank : (b + 1) * i_bank],
+                    op=ALU.add,
+                )
+            neg_max = soft.tile([P, TOKENS], F32)
+            nc.vector.tensor_reduce(out=neg_max[:], in_=s_ji[:], axis=mybir.AxisListType.X, op=ALU.max, negate=True)
+            row_tiles.append({"s_ji": s_ji, "neg_max": neg_max})
+
+        def exponentials(rt):
+            t = row_tiles[rt]
+            t["e_ji"] = soft.tile([P, TOKENS, TOKENS], F32, name="e_ji")
+            t["sums"] = soft.tile([P, TOKENS], F32, name="sums")
+            for j in range(TOKENS):
+                nc.scalar.activation(
+                    out=t["e_ji"][:, j, :],
+                    in_=t["s_ji"][:, j, :],
+                    func=EXP,
+                    bias=t["neg_max"][:, j : j + 1],
+                    scale=1.0,
+                    accum_out=t["sums"][:, j : j + 1],
+                )
+
+        def normalise(rt):
+            t = row_tiles[rt]
+            inv = soft.tile([P, TOKENS], F32)
+            nc.vector.reciprocal(out=inv[:], in_=t["sums"][:])
+            o_ij = soft.tile([P, TOKENS, TOKENS], F32)
+            nc.gpsimd.tensor_tensor(
+                out=o_ij[:],
+                in0=t["e_ji"][:].rearrange("p j i -> p i j"),
+                in1=inv[:].unsqueeze(1).to_broadcast([P, TOKENS, TOKENS]),
+                op=ALU.mult,
+            )
+            nc.sync.dma_start(out=out_rows[rt * P : (rt + 1) * P, :], in_=o_ij[:].rearrange("p i j -> p (i j)"))
+
+        prepare_wc()
+        for k in range(2):
+            channels_to_partitions(k)
+            quantise_x(k)
+            compress(k)
+        flatten(0)
+        nc.scalar.copy(out=bg_ji[:], in_=bg_all[:].rearrange("p (i j) -> p j i", j=TOKENS))
+        prepare_wg()
+        channels_to_partitions(2)
+        logits(0)
+        quantise_x(2)
+        compress(2)
+
+        for rt in range(ALL_ROW_TILES):
+            k = rt + LEAD
+            if rt + 1 < ALL_ROW_TILES and (rt + 1) % ROW_TILES == 0:
+                flatten((rt + 1) // ROW_TILES)
+            if k < HALVES:
+                channels_to_partitions(k)
+            exponentials(rt)
+            if rt > 0:
+                normalise(rt - 1)
+            if k < HALVES:
+                quantise_x(k)
+            if rt + 1 < ALL_ROW_TILES:
+                logits(rt + 1)
+            if k < HALVES:
+                compress(k)
+        normalise(ALL_ROW_TILES - 1)

@@ -207,7 +207,6 @@ def tile_dynamixerblock_pa_kernel(tc, x_seq, Wc, bc, Wg, bg, out):
         def exponentials(rt):
             t = row_tiles[rt]
             t["e_ji"] = soft.tile([P, TOKENS, TOKENS], F32, name="e_ji")
-            t["sums"] = soft.tile([P, TOKENS], F32, name="sums")
             for j in range(TOKENS):
                 nc.scalar.activation(
                     out=t["e_ji"][:, j, :],
@@ -215,13 +214,14 @@ def tile_dynamixerblock_pa_kernel(tc, x_seq, Wc, bc, Wg, bg, out):
                     func=EXP,
                     bias=t["neg_max"][:, j : j + 1],
                     scale=1.0,
-                    accum_out=t["sums"][:, j : j + 1],
                 )
 
         def normalise(rt):
             t = row_tiles[rt]
+            sums = soft.tile([P, TOKENS], F32)
+            nc.vector.tensor_reduce(out=sums[:], in_=t["e_ji"][:], axis=mybir.AxisListType.X, op=ALU.add)
             inv = soft.tile([P, TOKENS], F32)
-            nc.vector.reciprocal(out=inv[:], in_=t["sums"][:])
+            nc.vector.reciprocal(out=inv[:], in_=sums[:])
             o_ij = soft.tile([P, TOKENS, TOKENS], F32)
             nc.gpsimd.tensor_tensor(
                 out=o_ij[:],

@@ -207,6 +207,7 @@ def tile_dynamixerblock_pa_kernel(tc, x_seq, Wc, bc, Wg, bg, out):
         def exponentials(rt):
             t = row_tiles[rt]
             t["e_ji"] = soft.tile([P, TOKENS, TOKENS], F32, name="e_ji")
+            t["sums"] = soft.tile([P, TOKENS], F32, name="sums")
             for j in range(TOKENS):
                 nc.scalar.activation(
                     out=t["e_ji"][:, j, :],
@@ -214,16 +215,15 @@ def tile_dynamixerblock_pa_kernel(tc, x_seq, Wc, bc, Wg, bg, out):
                     func=EXP,
                     bias=t["neg_max"][:, j : j + 1],
                     scale=1.0,
+                    accum_out=t["sums"][:, j : j + 1],
                 )
 
         def normalise(rt):
             t = row_tiles[rt]
-            sums = soft.tile([P, TOKENS], F32)
-            nc.vector.tensor_reduce(out=sums[:], in_=t["e_ji"][:], axis=mybir.AxisListType.X, op=ALU.add)
             inv = soft.tile([P, TOKENS], F32)
-            nc.vector.reciprocal(out=inv[:], in_=sums[:])
+            nc.vector.reciprocal(out=inv[:], in_=t["sums"][:])
             o_ij = soft.tile([P, TOKENS, TOKENS], F32)
-            nc.gpsimd.tensor_tensor(
+            nc.vector.tensor_tensor(
                 out=o_ij[:],
                 in0=t["e_ji"][:].rearrange("p j i -> p i j"),
                 in1=inv[:].unsqueeze(1).to_broadcast([P, TOKENS, TOKENS]),

@@ -28,7 +28,7 @@ ALL_ROW_TILES = GROUPS * ROW_TILES
 WORDS = CHANNELS // 2
 HALF_TOKENS = BANK // P
 HALVES = GROUPS * Q_TOKENS // HALF_TOKENS
-LEAD = 3
+AHEAD = 3
 
 FLOPS = 2 * SEQS * TOKENS * CHANNELS * HEADS * REDUCED + 2 * SEQS * HEADS * TOKENS * REDUCED * MIX
 
@@ -60,7 +60,6 @@ def tile_dynamixerblock_pa_kernel(tc, x_seq, Wc, bc, Wg, bg, out):
         work = ctx.enter_context(tc.tile_pool(name="work", bufs=2))
         soft = ctx.enter_context(tc.tile_pool(name="soft", bufs=3))
         psum = ctx.enter_context(tc.psum_pool(name="psum", bufs=1))
-        ctx.enter_context(tc.manual_schedule())
 
         wc_sb = const.tile([P, CHANNELS], BF16)
         nc.sync.dma_start(out=wc_sb[:], in_=Wc)
@@ -100,7 +99,7 @@ def tile_dynamixerblock_pa_kernel(tc, x_seq, Wc, bc, Wg, bg, out):
 
         def prepare_wc():
             wc_words = wc_sb[:].bitcast(F32)
-            wc_T = psum.tile([P, 2, P], F32, tag="xT", bufs=2)
+            wc_T = psum.tile([P, 2, P], F32, tag="xT", bufs=4)
             for u in range(2):
                 nc.tensor.transpose(wc_T[:, u, :], wc_words[:, u * P : (u + 1) * P], ident_f32[:])
             wc_grp = const.tile([P, P * PACK], BF16, align_bytes=64)
@@ -113,7 +112,7 @@ def tile_dynamixerblock_pa_kernel(tc, x_seq, Wc, bc, Wg, bg, out):
         def prepare_wg():
             wg_grp = const.tile([P, MIX, PACK], BF16, align_bytes=64)
             for pair in range(MIX // P // 2):
-                wg_T = psum.tile([P, 2, PACK, P], BF16, tag="xT", bufs=2)
+                wg_T = psum.tile([P, 2, PACK, P], BF16, tag="xT", bufs=4)
                 for s in range(2):
                     for t in range(PACK):
                         nc.tensor.transpose(
@@ -137,14 +136,14 @@ def tile_dynamixerblock_pa_kernel(tc, x_seq, Wc, bc, Wg, bg, out):
                         "x_codes": work.tile([P, Q_TOKENS * P], U32, align_bytes=64, name="x_codes"),
                         "x_scales": work.tile([P, Q_TOKENS * P], U8, align_bytes=64, name="x_scales"),
                         "v_nat": work.tile([P, HEADS, Q_TOKENS, REDUCED], BF16, name="v_nat"),
-                        "v_codes": work.tile([P, GROUP_SEQS * HEADS], U32, align_bytes=64, name="v_codes"),
-                        "v_scales": work.tile([P, GROUP_SEQS * HEADS], U8, align_bytes=64, name="v_scales"),
+                        "v_codes": work.tile([P, GROUP_SEQS * HEADS], U32, align_bytes=64, name="v_codes", bufs=GROUPS),
+                        "v_scales": work.tile([P, GROUP_SEQS * HEADS], U8, align_bytes=64, name="v_scales", bufs=GROUPS),
                     }
                 )
             x_words = x_sb[g][:].bitcast(F32)
             x_grp_words = group_tiles[g]["x_grp"][:].bitcast(F32).rearrange("p (l m u) -> p l m u", l=Q_TOKENS, u=2)
             for pair in range(2 * part, 2 * part + 2):
-                x_T = psum.tile([P, 2, 2, P], F32, tag="xT", bufs=2)
+                x_T = psum.tile([P, 2, 2, P], F32, tag="xT", bufs=4)
                 for l2 in range(2):
                     for u in range(2):
                         first = (2 * pair + l2) * WORDS + u * P
@@ -191,7 +190,7 @@ def tile_dynamixerblock_pa_kernel(tc, x_seq, Wc, bc, Wg, bg, out):
             s_ji = soft.tile([P, TOKENS, TOKENS], F32)
             i_bank = BANK // TOKENS
             for b in range(MIX // BANK):
-                g_ps = psum.tile([P, BANK], F32, tag="g", bufs=4)
+                g_ps = psum.tile([P, BANK], F32, tag="g", bufs=2)
                 o_cols = slice(b * BANK, (b + 1) * BANK)
                 mx_pass(nc, g_ps[:], t["v_codes"][:, rows], t["v_scales"][:, rows], wg_codes[:, o_cols], wg_scales[:, o_cols])
                 nc.vector.tensor_tensor(
@@ -223,7 +222,8 @@ def tile_dynamixerblock_pa_kernel(tc, x_seq, Wc, bc, Wg, bg, out):
             inv = soft.tile([P, TOKENS], F32)
             nc.vector.reciprocal(out=inv[:], in_=t["sums"][:])
             o_ij = soft.tile([P, TOKENS, TOKENS], F32)
-            nc.vector.tensor_tensor(
+            engine = nc.vector if rt // ROW_TILES == GROUPS - 1 else nc.gpsimd
+            engine.tensor_tensor(
                 out=o_ij[:],
                 in0=t["e_ji"][:].rearrange("p j i -> p i j"),
                 in1=inv[:].unsqueeze(1).to_broadcast([P, TOKENS, TOKENS]),
@@ -231,32 +231,23 @@ def tile_dynamixerblock_pa_kernel(tc, x_seq, Wc, bc, Wg, bg, out):
             )
             nc.sync.dma_start(out=out_rows[rt * P : (rt + 1) * P, :], in_=o_ij[:].rearrange("p i j -> p (i j)"))
 
-        prepare_wc()
-        for k in range(2):
+        def front_half(k):
             channels_to_partitions(k)
             quantise_x(k)
             compress(k)
-        flatten(0)
-        nc.scalar.copy(out=bg_ji[:], in_=bg_all[:].rearrange("p (i j) -> p j i", j=TOKENS))
-        prepare_wg()
-        channels_to_partitions(2)
-        logits(0)
-        quantise_x(2)
-        compress(2)
+            if k % 2 == 1:
+                flatten(k // 2)
 
+        prepare_wc()
+        nc.gpsimd.tensor_copy(out=bg_ji[:], in_=bg_all[:].rearrange("p (i j) -> p j i", j=TOKENS))
+        front_half(0)
+        front_half(1)
+        prepare_wg()
+        for k in range(2, 2 + AHEAD):
+            front_half(k)
         for rt in range(ALL_ROW_TILES):
-            k = rt + LEAD
-            if rt + 1 < ALL_ROW_TILES and (rt + 1) % ROW_TILES == 0:
-                flatten((rt + 1) // ROW_TILES)
-            if k < HALVES:
-                channels_to_partitions(k)
+            logits(rt)
             exponentials(rt)
-            if rt > 0:
-                normalise(rt - 1)
-            if k < HALVES:
-                quantise_x(k)
-            if rt + 1 < ALL_ROW_TILES:
-                logits(rt + 1)
-            if k < HALVES:
-                compress(k)
-        normalise(ALL_ROW_TILES - 1)
+            normalise(rt)
+            if rt + 2 + AHEAD < HALVES:
+                front_half(rt + 2 + AHEAD)

@@ -28,7 +28,7 @@ ALL_ROW_TILES = GROUPS * ROW_TILES
 WORDS = CHANNELS // 2
 HALF_TOKENS = BANK // P
 HALVES = GROUPS * Q_TOKENS // HALF_TOKENS
-AHEAD = 3
+AHEAD = 2
 
 FLOPS = 2 * SEQS * TOKENS * CHANNELS * HEADS * REDUCED + 2 * SEQS * HEADS * TOKENS * REDUCED * MIX
 
@@ -99,7 +99,7 @@ def tile_dynamixerblock_pa_kernel(tc, x_seq, Wc, bc, Wg, bg, out):
 
         def prepare_wc():
             wc_words = wc_sb[:].bitcast(F32)
-            wc_T = psum.tile([P, 2, P], F32, tag="xT", bufs=4)
+            wc_T = psum.tile([P, 2, P], F32, tag="xT", bufs=3)
             for u in range(2):
                 nc.tensor.transpose(wc_T[:, u, :], wc_words[:, u * P : (u + 1) * P], ident_f32[:])
             wc_grp = const.tile([P, P * PACK], BF16, align_bytes=64)
@@ -112,7 +112,7 @@ def tile_dynamixerblock_pa_kernel(tc, x_seq, Wc, bc, Wg, bg, out):
         def prepare_wg():
             wg_grp = const.tile([P, MIX, PACK], BF16, align_bytes=64)
             for pair in range(MIX // P // 2):
-                wg_T = psum.tile([P, 2, PACK, P], BF16, tag="xT", bufs=4)
+                wg_T = psum.tile([P, 2, PACK, P], BF16, tag="xT", bufs=3)
                 for s in range(2):
                     for t in range(PACK):
                         nc.tensor.transpose(
@@ -143,7 +143,7 @@ def tile_dynamixerblock_pa_kernel(tc, x_seq, Wc, bc, Wg, bg, out):
             x_words = x_sb[g][:].bitcast(F32)
             x_grp_words = group_tiles[g]["x_grp"][:].bitcast(F32).rearrange("p (l m u) -> p l m u", l=Q_TOKENS, u=2)
             for pair in range(2 * part, 2 * part + 2):
-                x_T = psum.tile([P, 2, 2, P], F32, tag="xT", bufs=4)
+                x_T = psum.tile([P, 2, 2, P], F32, tag="xT", bufs=3)
                 for l2 in range(2):
                     for u in range(2):
                         first = (2 * pair + l2) * WORDS + u * P
@@ -190,7 +190,7 @@ def tile_dynamixerblock_pa_kernel(tc, x_seq, Wc, bc, Wg, bg, out):
             s_ji = soft.tile([P, TOKENS, TOKENS], F32)
             i_bank = BANK // TOKENS
             for b in range(MIX // BANK):
-                g_ps = psum.tile([P, BANK], F32, tag="g", bufs=2)
+                g_ps = psum.tile([P, BANK], F32, tag="g", bufs=3)
                 o_cols = slice(b * BANK, (b + 1) * BANK)
                 mx_pass(nc, g_ps[:], t["v_codes"][:, rows], t["v_scales"][:, rows], wg_codes[:, o_cols], wg_scales[:, o_cols])
                 nc.vector.tensor_tensor(

@@ -28,7 +28,7 @@ ALL_ROW_TILES = GROUPS * ROW_TILES
 WORDS = CHANNELS // 2
 HALF_TOKENS = BANK // P
 HALVES = GROUPS * Q_TOKENS // HALF_TOKENS
-AHEAD = 2
+AHEAD = 3
 
 FLOPS = 2 * SEQS * TOKENS * CHANNELS * HEADS * REDUCED + 2 * SEQS * HEADS * TOKENS * REDUCED * MIX
 
@@ -61,6 +61,9 @@ def tile_dynamixerblock_pa_kernel(tc, x_seq, Wc, bc, Wg, bg, out):
         soft = ctx.enter_context(tc.tile_pool(name="soft", bufs=3))
         psum = ctx.enter_context(tc.psum_pool(name="psum", bufs=1))
 
+        bias_row = const.tile([P, MIX + 2 * P], BF16)
+        nc.vector.memset(bias_row[:], 0.0)
+
         wc_sb = const.tile([P, CHANNELS], BF16)
         nc.sync.dma_start(out=wc_sb[:], in_=Wc)
         wg_sb = const.tile([P, MIX // P, TOKENS * REDUCED], BF16)
@@ -73,12 +76,14 @@ def tile_dynamixerblock_pa_kernel(tc, x_seq, Wc, bc, Wg, bg, out):
                     out=x_sb[g][:, part * half_row : (part + 1) * half_row],
                     in_=x_rows[g * P : (g + 1) * P, part * half_row : (part + 1) * half_row],
                 )
+                if g == 0 and part == 0:
+                    nc.sync.dma_start(out=bias_row[0:1, :MIX], in_=bg.unsqueeze(0))
+                    nc.sync.dma_start(out=bias_row[0:1, MIX : MIX + P], in_=bc.unsqueeze(0))
             if g == 0:
                 nc.sync.dma_start(out=wg_sb[:], in_=Wg.rearrange("(s p) k -> p s k", p=P))
-        bc_all = const.tile([P, HEADS * REDUCED], BF16)
-        nc.scalar.dma_start(out=bc_all[:], in_=bc.partition_broadcast(P))
-        bg_all = const.tile([P, MIX], BF16)
-        nc.scalar.dma_start(out=bg_all[:], in_=bg.partition_broadcast(P))
+        ones = const.tile([P, P], BF16)
+        nc.vector.memset(ones[:], 1.0)
+        bc_all = const.tile([P, HEADS * REDUCED], F32)
         bc_hlr = (
             bc_all[:]
             .rearrange("p (h r) -> p h r", h=HEADS)
@@ -97,9 +102,21 @@ def tile_dynamixerblock_pa_kernel(tc, x_seq, Wc, bc, Wg, bg, out):
         wg_scales = const.tile([P, MIX], U8, align_bytes=64)
         bg_ji = const.tile([P, TOKENS, TOKENS], F32)
 
+        def spread_biases():
+            i_bank = BANK // TOKENS
+            for b in range(MIX // BANK):
+                bg_ps = psum.tile([P, BANK], F32, tag="g", bufs=2)
+                nc.tensor.matmul(out=bg_ps[:], lhsT=ones[:], rhs=bias_row[:, b * BANK : (b + 1) * BANK], start=True, stop=True)
+                nc.scalar.copy(
+                    out=bg_ji[:, :, b * i_bank : (b + 1) * i_bank], in_=bg_ps[:].rearrange("p (i j) -> p j i", j=TOKENS)
+                )
+            bc_ps = psum.tile([P, 2 * P], F32, tag="g", bufs=2)
+            nc.tensor.matmul(out=bc_ps[:], lhsT=ones[:], rhs=bias_row[:, MIX:], start=True, stop=True)
+            nc.vector.tensor_copy(out=bc_all[:], in_=bc_ps[:, :P])
+
         def prepare_wc():
             wc_words = wc_sb[:].bitcast(F32)
-            wc_T = psum.tile([P, 2, P], F32, tag="xT", bufs=3)
+            wc_T = psum.tile([P, 2, P], F32, tag="xT", bufs=4)
             for u in range(2):
                 nc.tensor.transpose(wc_T[:, u, :], wc_words[:, u * P : (u + 1) * P], ident_f32[:])
             wc_grp = const.tile([P, P * PACK], BF16, align_bytes=64)
@@ -112,7 +129,7 @@ def tile_dynamixerblock_pa_kernel(tc, x_seq, Wc, bc, Wg, bg, out):
         def prepare_wg():
             wg_grp = const.tile([P, MIX, PACK], BF16, align_bytes=64)
             for pair in range(MIX // P // 2):
-                wg_T = psum.tile([P, 2, PACK, P], BF16, tag="xT", bufs=3)
+                wg_T = psum.tile([P, 2, PACK, P], BF16, tag="xT", bufs=4)
                 for s in range(2):
                     for t in range(PACK):
                         nc.tensor.transpose(
@@ -143,7 +160,7 @@ def tile_dynamixerblock_pa_kernel(tc, x_seq, Wc, bc, Wg, bg, out):
             x_words = x_sb[g][:].bitcast(F32)
             x_grp_words = group_tiles[g]["x_grp"][:].bitcast(F32).rearrange("p (l m u) -> p l m u", l=Q_TOKENS, u=2)
             for pair in range(2 * part, 2 * part + 2):
-                x_T = psum.tile([P, 2, 2, P], F32, tag="xT", bufs=3)
+                x_T = psum.tile([P, 2, 2, P], F32, tag="xT", bufs=4)
                 for l2 in range(2):
                     for u in range(2):
                         first = (2 * pair + l2) * WORDS + u * P
@@ -190,7 +207,7 @@ def tile_dynamixerblock_pa_kernel(tc, x_seq, Wc, bc, Wg, bg, out):
             s_ji = soft.tile([P, TOKENS, TOKENS], F32)
             i_bank = BANK // TOKENS
             for b in range(MIX // BANK):
-                g_ps = psum.tile([P, BANK], F32, tag="g", bufs=3)
+                g_ps = psum.tile([P, BANK], F32, tag="g", bufs=2)
                 o_cols = slice(b * BANK, (b + 1) * BANK)
                 mx_pass(nc, g_ps[:], t["v_codes"][:, rows], t["v_scales"][:, rows], wg_codes[:, o_cols], wg_scales[:, o_cols])
                 nc.vector.tensor_tensor(
@@ -223,12 +240,13 @@ def tile_dynamixerblock_pa_kernel(tc, x_seq, Wc, bc, Wg, bg, out):
             nc.vector.reciprocal(out=inv[:], in_=t["sums"][:])
             o_ij = soft.tile([P, TOKENS, TOKENS], F32)
             engine = nc.vector if rt // ROW_TILES == GROUPS - 1 else nc.gpsimd
-            engine.tensor_tensor(
-                out=o_ij[:],
-                in0=t["e_ji"][:].rearrange("p j i -> p i j"),
-                in1=inv[:].unsqueeze(1).to_broadcast([P, TOKENS, TOKENS]),
-                op=ALU.mult,
-            )
+            for i_half in (slice(0, TOKENS // 2), slice(TOKENS // 2, TOKENS)):
+                engine.tensor_tensor(
+                    out=o_ij[:, i_half, :],
+                    in0=t["e_ji"][:, :, i_half].rearrange("p j i -> p i j"),
+                    in1=inv[:].unsqueeze(1).to_broadcast([P, TOKENS // 2, TOKENS]),
+                    op=ALU.mult,
+                )
             nc.sync.dma_start(out=out_rows[rt * P : (rt + 1) * P, :], in_=o_ij[:].rearrange("p i j -> p (i j)"))
 
         def front_half(k):
@@ -239,9 +257,13 @@ def tile_dynamixerblock_pa_kernel(tc, x_seq, Wc, bc, Wg, bg, out):
                 flatten(k // 2)
 
         prepare_wc()
-        nc.gpsimd.tensor_copy(out=bg_ji[:], in_=bg_all[:].rearrange("p (i j) -> p j i", j=TOKENS))
-        front_half(0)
-        front_half(1)
+        channels_to_partitions(0)
+        channels_to_partitions(1)
+        spread_biases()
+        for k in range(2):
+            quantise_x(k)
+            compress(k)
+        flatten(0)
         prepare_wg()
         for k in range(2, 2 + AHEAD):
             front_half(k)

@@ -28,6 +28,8 @@ ALL_ROW_TILES = GROUPS * ROW_TILES
 WORDS = CHANNELS // 2
 HALF_TOKENS = BANK // P
 HALVES = GROUPS * Q_TOKENS // HALF_TOKENS
+STORE_I = TOKENS // 2
+PIECE_I = TOKENS // 4
 AHEAD = 3
 
 FLOPS = 2 * SEQS * TOKENS * CHANNELS * HEADS * REDUCED + 2 * SEQS * HEADS * TOKENS * REDUCED * MIX
@@ -64,6 +66,10 @@ def tile_dynamixerblock_pa_kernel(tc, x_seq, Wc, bc, Wg, bg, out):
         bias_row = const.tile([P, MIX + 2 * P], BF16)
         nc.vector.memset(bias_row[:], 0.0)
 
+        table_warmer = const.tile([P, 1], F32)
+        nc.vector.memset(table_warmer[:], 0.0)
+        nc.scalar.activation(out=table_warmer[:], in_=table_warmer[:], func=EXP)
+
         wc_sb = const.tile([P, CHANNELS], BF16)
         nc.sync.dma_start(out=wc_sb[:], in_=Wc)
         wg_sb = const.tile([P, MIX // P, TOKENS * REDUCED], BF16)
@@ -80,7 +86,9 @@ def tile_dynamixerblock_pa_kernel(tc, x_seq, Wc, bc, Wg, bg, out):
                     nc.sync.dma_start(out=bias_row[0:1, :MIX], in_=bg.unsqueeze(0))
                     nc.sync.dma_start(out=bias_row[0:1, MIX : MIX + P], in_=bc.unsqueeze(0))
             if g == 0:
-                nc.sync.dma_start(out=wg_sb[:], in_=Wg.rearrange("(s p) k -> p s k", p=P))
+                wg_slabs = Wg.rearrange("(s p) k -> p s k", p=P)
+                for slabs in (slice(0, MIX // P // 2), slice(MIX // P // 2, MIX // P)):
+                    nc.sync.dma_start(out=wg_sb[:, slabs, :], in_=wg_slabs[:, slabs, :])
         ones = const.tile([P, P], BF16)
         nc.vector.memset(ones[:], 1.0)
         bc_all = const.tile([P, HEADS * REDUCED], F32)
@@ -240,14 +248,18 @@ def tile_dynamixerblock_pa_kernel(tc, x_seq, Wc, bc, Wg, bg, out):
             nc.vector.reciprocal(out=inv[:], in_=t["sums"][:])
             o_ij = soft.tile([P, TOKENS, TOKENS], F32)
             engine = nc.vector if rt // ROW_TILES == GROUPS - 1 else nc.gpsimd
-            for i_half in (slice(0, TOKENS // 2), slice(TOKENS // 2, TOKENS)):
-                engine.tensor_tensor(
-                    out=o_ij[:, i_half, :],
-                    in0=t["e_ji"][:, :, i_half].rearrange("p j i -> p i j"),
-                    in1=inv[:].unsqueeze(1).to_broadcast([P, TOKENS // 2, TOKENS]),
-                    op=ALU.mult,
+            for i_store in range(0, TOKENS, STORE_I):
+                for i_first in range(i_store, i_store + STORE_I, PIECE_I):
+                    engine.tensor_tensor(
+                        out=o_ij[:, i_first : i_first + PIECE_I, :],
+                        in0=t["e_ji"][:, :, i_first : i_first + PIECE_I].rearrange("p j i -> p i j"),
+                        in1=inv[:].unsqueeze(1).to_broadcast([P, PIECE_I, TOKENS]),
+                        op=ALU.mult,
+                    )
+                nc.sync.dma_start(
+                    out=out_rows[rt * P : (rt + 1) * P, i_store * TOKENS : (i_store + STORE_I) * TOKENS],
+                    in_=o_ij[:, i_store : i_store + STORE_I, :].rearrange("p i j -> p (i j)"),
                 )
-            nc.sync.dma_start(out=out_rows[rt * P : (rt + 1) * P, :], in_=o_ij[:].rearrange("p i j -> p (i j)"))
 
         def front_half(k):
             channels_to_partitions(k)

@@ -28,8 +28,6 @@ ALL_ROW_TILES = GROUPS * ROW_TILES
 WORDS = CHANNELS // 2
 HALF_TOKENS = BANK // P
 HALVES = GROUPS * Q_TOKENS // HALF_TOKENS
-STORE_I = TOKENS // 2
-PIECE_I = TOKENS // 4
 AHEAD = 3
 
 FLOPS = 2 * SEQS * TOKENS * CHANNELS * HEADS * REDUCED + 2 * SEQS * HEADS * TOKENS * REDUCED * MIX
@@ -66,10 +64,6 @@ def tile_dynamixerblock_pa_kernel(tc, x_seq, Wc, bc, Wg, bg, out):
         bias_row = const.tile([P, MIX + 2 * P], BF16)
         nc.vector.memset(bias_row[:], 0.0)
 
-        table_warmer = const.tile([P, 1], F32)
-        nc.vector.memset(table_warmer[:], 0.0)
-        nc.scalar.activation(out=table_warmer[:], in_=table_warmer[:], func=EXP)
-
         wc_sb = const.tile([P, CHANNELS], BF16)
         nc.sync.dma_start(out=wc_sb[:], in_=Wc)
         wg_sb = const.tile([P, MIX // P, TOKENS * REDUCED], BF16)
@@ -86,9 +80,7 @@ def tile_dynamixerblock_pa_kernel(tc, x_seq, Wc, bc, Wg, bg, out):
                     nc.sync.dma_start(out=bias_row[0:1, :MIX], in_=bg.unsqueeze(0))
                     nc.sync.dma_start(out=bias_row[0:1, MIX : MIX + P], in_=bc.unsqueeze(0))
             if g == 0:
-                wg_slabs = Wg.rearrange("(s p) k -> p s k", p=P)
-                for slabs in (slice(0, MIX // P // 2), slice(MIX // P // 2, MIX // P)):
-                    nc.sync.dma_start(out=wg_sb[:, slabs, :], in_=wg_slabs[:, slabs, :])
+                nc.sync.dma_start(out=wg_sb[:], in_=Wg.rearrange("(s p) k -> p s k", p=P))
         ones = const.tile([P, P], BF16)
         nc.vector.memset(ones[:], 1.0)
         bc_all = const.tile([P, HEADS * REDUCED], F32)
@@ -203,7 +195,7 @@ def tile_dynamixerblock_pa_kernel(tc, x_seq, Wc, bc, Wg, bg, out):
             for h in range(HEADS):
                 nc.tensor.transpose(v_T[:, :, h, :], t["v_nat"][:, h, :, :].rearrange("p l r -> p (l r)"), ident_bf16[:])
             v_grp = work.tile([P, GROUP_SEQS * HEADS * PACK], BF16, align_bytes=64)
-            nc.vector.tensor_copy(out=v_grp[:], in_=v_T[:].rearrange("p n h a -> p (n h a)"))
+            nc.scalar.copy(out=v_grp[:], in_=v_T[:].rearrange("p n h a -> p (n h a)"))
             quantise(nc, t["v_codes"][:], t["v_scales"][:], v_grp[:])
 
         row_tiles = []
@@ -248,18 +240,14 @@ def tile_dynamixerblock_pa_kernel(tc, x_seq, Wc, bc, Wg, bg, out):
             nc.vector.reciprocal(out=inv[:], in_=t["sums"][:])
             o_ij = soft.tile([P, TOKENS, TOKENS], F32)
             engine = nc.vector if rt // ROW_TILES == GROUPS - 1 else nc.gpsimd
-            for i_store in range(0, TOKENS, STORE_I):
-                for i_first in range(i_store, i_store + STORE_I, PIECE_I):
-                    engine.tensor_tensor(
-                        out=o_ij[:, i_first : i_first + PIECE_I, :],
-                        in0=t["e_ji"][:, :, i_first : i_first + PIECE_I].rearrange("p j i -> p i j"),
-                        in1=inv[:].unsqueeze(1).to_broadcast([P, PIECE_I, TOKENS]),
-                        op=ALU.mult,
-                    )
-                nc.sync.dma_start(
-                    out=out_rows[rt * P : (rt + 1) * P, i_store * TOKENS : (i_store + STORE_I) * TOKENS],
-                    in_=o_ij[:, i_store : i_store + STORE_I, :].rearrange("p i j -> p (i j)"),
+            for i_half in (slice(0, TOKENS // 2), slice(TOKENS // 2, TOKENS)):
+                engine.tensor_tensor(
+                    out=o_ij[:, i_half, :],
+                    in0=t["e_ji"][:, :, i_half].rearrange("p j i -> p i j"),
+                    in1=inv[:].unsqueeze(1).to_broadcast([P, TOKENS // 2, TOKENS]),
+                    op=ALU.mult,
                 )
+            nc.sync.dma_start(out=out_rows[rt * P : (rt + 1) * P, :], in_=o_ij[:].rearrange("p i j -> p (i j)"))
 
         def front_half(k):
             channels_to_partitions(k)

@@ -240,13 +240,11 @@ def tile_dynamixerblock_pa_kernel(tc, x_seq, Wc, bc, Wg, bg, out):
             nc.vector.reciprocal(out=inv[:], in_=t["sums"][:])
             o_ij = soft.tile([P, TOKENS, TOKENS], F32)
             engine = nc.vector if rt // ROW_TILES == GROUPS - 1 else nc.gpsimd
-            for i_half in (slice(0, TOKENS // 2), slice(TOKENS // 2, TOKENS)):
-                engine.tensor_tensor(
-                    out=o_ij[:, i_half, :],
-                    in0=t["e_ji"][:, :, i_half].rearrange("p j i -> p i j"),
-                    in1=inv[:].unsqueeze(1).to_broadcast([P, TOKENS // 2, TOKENS]),
-                    op=ALU.mult,
-                )
+            o_blocks = o_ij[:].rearrange("p i (b q) -> p b i q", q=4)
+            e_blocks = t["e_ji"][:].rearrange("p (b q) i -> p b i q", q=4)
+            inv_blocks = inv[:].rearrange("p (b q) -> p b q", q=4).unsqueeze(2).to_broadcast([P, TOKENS // 4, TOKENS, 4])
+            for half in (slice(0, TOKENS // 8), slice(TOKENS // 8, TOKENS // 4)):
+                engine.tensor_tensor(out=o_blocks[:, half], in0=e_blocks[:, half], in1=inv_blocks[:, half], op=ALU.mult)
             nc.sync.dma_start(out=out_rows[rt * P : (rt + 1) * P, :], in_=o_ij[:].rearrange("p i j -> p (i j)"))
 
         def front_half(k):

@@ -28,6 +28,8 @@ ALL_ROW_TILES = GROUPS * ROW_TILES
 WORDS = CHANNELS // 2
 HALF_TOKENS = BANK // P
 HALVES = GROUPS * Q_TOKENS // HALF_TOKENS
+BANKS = MIX // BANK
+J_BANK = TOKENS // BANKS
 AHEAD = 3
 
 FLOPS = 2 * SEQS * TOKENS * CHANNELS * HEADS * REDUCED + 2 * SEQS * HEADS * TOKENS * REDUCED * MIX
@@ -127,20 +129,22 @@ def tile_dynamixerblock_pa_kernel(tc, x_seq, Wc, bc, Wg, bg, out):
             quantise(nc, wc_codes[:], wc_scales[:], wc_grp[:])
 
         def prepare_wg():
-            wg_grp = const.tile([P, MIX, PACK], BF16, align_bytes=64)
+            wg_grp = const.tile([P, BANKS, TOKENS, J_BANK, PACK], BF16, align_bytes=64)
+            i_pair = 2 * P // TOKENS
             for pair in range(MIX // P // 2):
-                wg_T = psum.tile([P, 2, PACK, P], BF16, tag="xT", bufs=4)
+                wg_T = psum.tile([P, PACK, 2, P], BF16, tag="xT", bufs=4)
                 for s in range(2):
                     for t in range(PACK):
                         nc.tensor.transpose(
-                            wg_T[:, s, t, :], wg_sb[:, 2 * pair + s, t * P : (t + 1) * P], ident_bf16[:]
+                            wg_T[:, t, s, :], wg_sb[:, 2 * pair + s, t * P : (t + 1) * P], ident_bf16[:]
                         )
-                grouped = wg_grp[:, 2 * pair * P : (2 * pair + 2) * P, :].rearrange("p (s o) t -> p s o t", s=2)
-                if pair % 2 == 0:
-                    nc.scalar.copy(out=grouped, in_=wg_T[:].rearrange("p s t o -> p s o t"))
-                else:
-                    nc.vector.tensor_copy(out=grouped, in_=wg_T[:].rearrange("p s t o -> p s o t"))
-            quantise(nc, wg_codes[:], wg_scales[:], wg_grp[:].rearrange("p o t -> p (o t)"))
+                by_bank = wg_T[:].rearrange("p t s (i b j) -> p b (s i) j t", b=BANKS, j=J_BANK)
+                for b in range(BANKS):
+                    copy = nc.scalar.copy if pair % 2 == 0 else nc.vector.tensor_copy
+                    copy(out=wg_grp[:, b, pair * i_pair : (pair + 1) * i_pair], in_=by_bank[:, b])
+            for b in range(BANKS):
+                cols = slice(b * BANK, (b + 1) * BANK)
+                quantise(nc, wg_codes[:, cols], wg_scales[:, cols], wg_grp[:, b].rearrange("p i j t -> p (i j t)"))
 
         group_tiles = []
 
@@ -205,45 +209,52 @@ def tile_dynamixerblock_pa_kernel(tc, x_seq, Wc, bc, Wg, bg, out):
             t = group_tiles[g]
             rows = slice(part * P, (part + 1) * P)
             s_ji = soft.tile([P, TOKENS, TOKENS], F32)
-            i_bank = BANK // TOKENS
-            for b in range(MIX // BANK):
+            neg_max = soft.tile([P, TOKENS], F32)
+            for b in range(BANKS):
                 g_ps = psum.tile([P, BANK], F32, tag="g", bufs=2)
                 o_cols = slice(b * BANK, (b + 1) * BANK)
+                js = slice(b * J_BANK, (b + 1) * J_BANK)
                 mx_pass(nc, g_ps[:], t["v_codes"][:, rows], t["v_scales"][:, rows], wg_codes[:, o_cols], wg_scales[:, o_cols])
                 nc.vector.tensor_tensor(
-                    out=s_ji[:, :, b * i_bank : (b + 1) * i_bank],
-                    in0=g_ps[:].rearrange("p (i j) -> p j i", j=TOKENS),
-                    in1=bg_ji[:, :, b * i_bank : (b + 1) * i_bank],
-                    op=ALU.add,
+                    out=s_ji[:, js, :], in0=g_ps[:].rearrange("p (i j) -> p j i", j=J_BANK), in1=bg_ji[:, js, :], op=ALU.add
                 )
-            neg_max = soft.tile([P, TOKENS], F32)
-            nc.vector.tensor_reduce(out=neg_max[:], in_=s_ji[:], axis=mybir.AxisListType.X, op=ALU.max, negate=True)
+                nc.vector.tensor_reduce(
+                    out=neg_max[:, js], in_=s_ji[:, js, :], axis=mybir.AxisListType.X, op=ALU.max, negate=True
+                )
             row_tiles.append({"s_ji": s_ji, "neg_max": neg_max})
 
         def exponentials(rt):
             t = row_tiles[rt]
-            t["e_ji"] = soft.tile([P, TOKENS, TOKENS], F32, name="e_ji")
-            t["sums"] = soft.tile([P, TOKENS], F32, name="sums")
-            for j in range(TOKENS):
+            e_ji = t["e_ji"] = soft.tile([P, TOKENS, TOKENS], F32, name="e_ji")
+            sums = t["sums"] = soft.tile([P, TOKENS], F32, name="sums")
+            for j in range(J_BANK):
                 nc.scalar.activation(
-                    out=t["e_ji"][:, j, :],
+                    out=e_ji[:, j, :],
                     in_=t["s_ji"][:, j, :],
                     func=EXP,
                     bias=t["neg_max"][:, j : j + 1],
                     scale=1.0,
-                    accum_out=t["sums"][:, j : j + 1],
+                    accum_out=sums[:, j : j + 1],
                 )
+            for j in range(J_BANK, TOKENS):
+                nc.scalar.activation(
+                    out=e_ji[:, j, :], in_=t["s_ji"][:, j, :], func=EXP, bias=t["neg_max"][:, j : j + 1], scale=1.0
+                )
+            js = slice(J_BANK, TOKENS)
+            nc.vector.tensor_reduce(out=sums[:, js], in_=e_ji[:, js, :], axis=mybir.AxisListType.X, op=ALU.add)
 
         def normalise(rt):
             t = row_tiles[rt]
             inv = soft.tile([P, TOKENS], F32)
-            nc.vector.reciprocal(out=inv[:], in_=t["sums"][:])
             o_ij = soft.tile([P, TOKENS, TOKENS], F32)
             engine = nc.vector if rt // ROW_TILES == GROUPS - 1 else nc.gpsimd
             o_blocks = o_ij[:].rearrange("p i (b q) -> p b i q", q=4)
             e_blocks = t["e_ji"][:].rearrange("p (b q) i -> p b i q", q=4)
             inv_blocks = inv[:].rearrange("p (b q) -> p b q", q=4).unsqueeze(2).to_broadcast([P, TOKENS // 4, TOKENS, 4])
-            for half in (slice(0, TOKENS // 8), slice(TOKENS // 8, TOKENS // 4)):
+            for b in range(BANKS):
+                js = slice(b * J_BANK, (b + 1) * J_BANK)
+                nc.vector.reciprocal(out=inv[:, js], in_=t["sums"][:, js])
+                half = slice(b * J_BANK // 4, (b + 1) * J_BANK // 4)
                 engine.tensor_tensor(out=o_blocks[:, half], in0=e_blocks[:, half], in1=inv_blocks[:, half], op=ALU.mult)
             nc.sync.dma_start(out=out_rows[rt * P : (rt + 1) * P, :], in_=o_ij[:].rearrange("p i j -> p (i j)"))
 

from contextlib import ExitStack

import concourse.mybir as mybir
from concourse.masks import make_identity

F32 = mybir.dt.float32
BF16 = mybir.dt.bfloat16
U32 = mybir.dt.uint32
U8 = mybir.dt.uint8
FP8X4 = mybir.dt.float8_e4m3fn_x4
ALU = mybir.AluOpType
EXP = mybir.ActivationFunctionType.Exp

P = 128
PACK = 4
BANK = 512

SEQS, TOKENS, CHANNELS = 128, 32, 512
HEADS, REDUCED = 8, 16
MIX = TOKENS * TOKENS

QUARTERS = PACK
Q_TOKENS = TOKENS // QUARTERS
GROUP_SEQS = P // QUARTERS
GROUPS = SEQS // GROUP_SEQS
ROW_TILES = GROUP_SEQS * HEADS // P
ALL_ROW_TILES = GROUPS * ROW_TILES
WORDS = CHANNELS // 2
HALF_TOKENS = BANK // P
HALVES = GROUPS * Q_TOKENS // HALF_TOKENS
BANKS = MIX // BANK
J_BANK = TOKENS // BANKS
AHEAD = 3

FLOPS = 2 * SEQS * TOKENS * CHANNELS * HEADS * REDUCED + 2 * SEQS * HEADS * TOKENS * REDUCED * MIX


def quantise(nc, codes, scales, grouped):
    nc.vector.quantize_mx(out=codes.bitcast(FP8X4), scales=scales, in_=grouped)


def mx_pass(nc, acc, lhsT, lhsT_scale, rhs, rhs_scale):
    nc.tensor.matmul_mx(
        out=acc,
        lhsT=lhsT.bitcast(FP8X4),
        lhsT_scale=lhsT_scale,
        rhs=rhs.bitcast(FP8X4),
        rhs_scale=rhs_scale,
        start=True,
        stop=True,
    )


def tile_dynamixerblock_pa_kernel(tc, x_seq, Wc, bc, Wg, bg, out):
    nc = tc.nc
    x_rows = x_seq.rearrange("n (a l) c -> (n a) (l c)", a=QUARTERS)
    out_rows = out.rearrange("n h i j -> (n h) (i j)")

    with ExitStack() as ctx:
        const = ctx.enter_context(tc.tile_pool(name="const", bufs=1))
        xin = ctx.enter_context(tc.tile_pool(name="xin", bufs=GROUPS))
        work = ctx.enter_context(tc.tile_pool(name="work", bufs=2))
        soft = ctx.enter_context(tc.tile_pool(name="soft", bufs=3))
        psum = ctx.enter_context(tc.psum_pool(name="psum", bufs=1))

        bias_row = const.tile([P, MIX + 2 * P], BF16)
        nc.vector.memset(bias_row[:], 0.0)

        wc_sb = const.tile([P, CHANNELS], BF16)
        nc.sync.dma_start(out=wc_sb[:], in_=Wc)
        wg_sb = const.tile([P, MIX // P, TOKENS * REDUCED], BF16)
        x_sb = []
        half_row = HALF_TOKENS * CHANNELS
        for g in range(GROUPS):
            x_sb.append(xin.tile([P, Q_TOKENS * CHANNELS], BF16, name="x_sb"))
            for part in range(2):
                nc.sync.dma_start(
                    out=x_sb[g][:, part * half_row : (part + 1) * half_row],
                    in_=x_rows[g * P : (g + 1) * P, part * half_row : (part + 1) * half_row],
                )
                if g == 0 and part == 0:
                    nc.sync.dma_start(out=bias_row[0:1, :MIX], in_=bg.unsqueeze(0))
                    nc.sync.dma_start(out=bias_row[0:1, MIX : MIX + P], in_=bc.unsqueeze(0))
            if g == 0:
                nc.sync.dma_start(out=wg_sb[:], in_=Wg.rearrange("(s p) k -> p s k", p=P))
        ones = const.tile([P, P], BF16)
        nc.vector.memset(ones[:], 1.0)
        bc_all = const.tile([P, HEADS * REDUCED], F32)
        bc_hlr = (
            bc_all[:]
            .rearrange("p (h r) -> p h r", h=HEADS)
            .unsqueeze(2)
            .to_broadcast([P, HEADS, HALF_TOKENS, REDUCED])
        )

        ident_f32 = const.tile([P, P], F32)
        make_identity(nc, ident_f32[:])
        ident_bf16 = const.tile([P, P], BF16)
        make_identity(nc, ident_bf16[:])

        wc_codes = const.tile([P, P], U32, align_bytes=64)
        wc_scales = const.tile([P, P], U8, align_bytes=64)
        wg_codes = const.tile([P, MIX], U32, align_bytes=64)
        wg_scales = const.tile([P, MIX], U8, align_bytes=64)
        bg_ji = const.tile([P, TOKENS, TOKENS], F32)

        def spread_biases():
            i_bank = BANK // TOKENS
            for b in range(MIX // BANK):
                bg_ps = psum.tile([P, BANK], F32, tag="g", bufs=2)
                nc.tensor.matmul(out=bg_ps[:], lhsT=ones[:], rhs=bias_row[:, b * BANK : (b + 1) * BANK], start=True, stop=True)
                nc.scalar.copy(
                    out=bg_ji[:, :, b * i_bank : (b + 1) * i_bank], in_=bg_ps[:].rearrange("p (i j) -> p j i", j=TOKENS)
                )
            bc_ps = psum.tile([P, 2 * P], F32, tag="g", bufs=2)
            nc.tensor.matmul(out=bc_ps[:], lhsT=ones[:], rhs=bias_row[:, MIX:], start=True, stop=True)
            nc.vector.tensor_copy(out=bc_all[:], in_=bc_ps[:, :P])

        def prepare_wc():
            wc_words = wc_sb[:].bitcast(F32)
            wc_T = psum.tile([P, 2, P], F32, tag="xT", bufs=4)
            for u in range(2):
                nc.tensor.transpose(wc_T[:, u, :], wc_words[:, u * P : (u + 1) * P], ident_f32[:])
            wc_grp = const.tile([P, P * PACK], BF16, align_bytes=64)
            nc.vector.tensor_copy(
                out=wc_grp[:].bitcast(F32).rearrange("p (m u) -> p m u", u=2),
                in_=wc_T[:].rearrange("p u m -> p m u"),
            )
            quantise(nc, wc_codes[:], wc_scales[:], wc_grp[:])

        def prepare_wg():
            wg_grp = const.tile([P, BANKS, TOKENS, J_BANK, PACK], BF16, align_bytes=64)
            i_pair = 2 * P // TOKENS
            for pair in range(MIX // P // 2):
                wg_T = psum.tile([P, PACK, 2, P], BF16, tag="xT", bufs=4)
                for s in range(2):
                    for t in range(PACK):
                        nc.tensor.transpose(
                            wg_T[:, t, s, :], wg_sb[:, 2 * pair + s, t * P : (t + 1) * P], ident_bf16[:]
                        )
                by_bank = wg_T[:].rearrange("p t s (i b j) -> p b (s i) j t", b=BANKS, j=J_BANK)
                for b in range(BANKS):
                    copy = nc.scalar.copy if pair % 2 == 0 else nc.vector.tensor_copy
                    copy(out=wg_grp[:, b, pair * i_pair : (pair + 1) * i_pair], in_=by_bank[:, b])
            for b in range(BANKS):
                cols = slice(b * BANK, (b + 1) * BANK)
                quantise(nc, wg_codes[:, cols], wg_scales[:, cols], wg_grp[:, b].rearrange("p i j t -> p (i j t)"))

        group_tiles = []

        def channels_to_partitions(k):
            g, part = divmod(k, 2)
            if part == 0:
                group_tiles.append(
                    {
                        "x_grp": work.tile([P, Q_TOKENS * P * PACK], BF16, align_bytes=64, name="x_grp"),
                        "x_codes": work.tile([P, Q_TOKENS * P], U32, align_bytes=64, name="x_codes"),
                        "x_scales": work.tile([P, Q_TOKENS * P], U8, align_bytes=64, name="x_scales"),
                        "v_nat": work.tile([P, HEADS, Q_TOKENS, REDUCED], BF16, name="v_nat"),
                        "v_codes": work.tile([P, GROUP_SEQS * HEADS], U32, align_bytes=64, name="v_codes", bufs=GROUPS),
                        "v_scales": work.tile([P, GROUP_SEQS * HEADS], U8, align_bytes=64, name="v_scales", bufs=GROUPS),
                    }
                )
            x_words = x_sb[g][:].bitcast(F32)
            x_grp_words = group_tiles[g]["x_grp"][:].bitcast(F32).rearrange("p (l m u) -> p l m u", l=Q_TOKENS, u=2)
            for pair in range(2 * part, 2 * part + 2):
                x_T = psum.tile([P, 2, 2, P], F32, tag="xT", bufs=4)
                for l2 in range(2):
                    for u in range(2):
                        first = (2 * pair + l2) * WORDS + u * P
                        nc.tensor.transpose(x_T[:, l2, u, :], x_words[:, first : first + P], ident_f32[:])
                nc.scalar.copy(out=x_grp_words[:, 2 * pair : 2 * pair + 2], in_=x_T[:].rearrange("p l u m -> p l m u"))

        def quantise_x(k):
            g, part = divmod(k, 2)
            t = group_tiles[g]
            cols = slice(part * BANK, (part + 1) * BANK)
            quantise(
                nc, t["x_codes"][:, cols], t["x_scales"][:, cols], t["x_grp"][:, part * BANK * PACK : (part + 1) * BANK * PACK]
            )

        def compress(k):
            g, part = divmod(k, 2)
            t = group_tiles[g]
            u_ps = psum.tile([P, HALF_TOKENS, P], F32, tag="u", bufs=1)
            for l4 in range(HALF_TOKENS):
                m = slice((HALF_TOKENS * part + l4) * P, (HALF_TOKENS * part + l4 + 1) * P)
                mx_pass(nc, u_ps[:, l4, :], t["x_codes"][:, m], t["x_scales"][:, m], wc_codes[:], wc_scales[:])
            nc.vector.tensor_tensor(
                out=t["v_nat"][:, :, HALF_TOKENS * part : HALF_TOKENS * (part + 1), :],
                in0=u_ps[:].rearrange("p l (h r) -> p h l r", h=HEADS),
                in1=bc_hlr,
                op=ALU.add,
            )

        def flatten(g):
            t = group_tiles[g]
            v_T = psum.tile([P, GROUP_SEQS, HEADS, QUARTERS], BF16, tag="vT", bufs=1)
            for h in range(HEADS):
                nc.tensor.transpose(v_T[:, :, h, :], t["v_nat"][:, h, :, :].rearrange("p l r -> p (l r)"), ident_bf16[:])
            v_grp = work.tile([P, GROUP_SEQS * HEADS * PACK], BF16, align_bytes=64)
            nc.scalar.copy(out=v_grp[:], in_=v_T[:].rearrange("p n h a -> p (n h a)"))
            quantise(nc, t["v_codes"][:], t["v_scales"][:], v_grp[:])

        row_tiles = []

        def logits(rt):
            g, part = divmod(rt, ROW_TILES)
            t = group_tiles[g]
            rows = slice(part * P, (part + 1) * P)
            s_ji = soft.tile([P, TOKENS, TOKENS], F32)
            neg_max = soft.tile([P, TOKENS], F32)
            for b in range(BANKS):
                g_ps = psum.tile([P, BANK], F32, tag="g", bufs=2)
                o_cols = slice(b * BANK, (b + 1) * BANK)
                js = slice(b * J_BANK, (b + 1) * J_BANK)
                mx_pass(nc, g_ps[:], t["v_codes"][:, rows], t["v_scales"][:, rows], wg_codes[:, o_cols], wg_scales[:, o_cols])
                nc.vector.tensor_tensor(
                    out=s_ji[:, js, :], in0=g_ps[:].rearrange("p (i j) -> p j i", j=J_BANK), in1=bg_ji[:, js, :], op=ALU.add
                )
                nc.vector.tensor_reduce(
                    out=neg_max[:, js], in_=s_ji[:, js, :], axis=mybir.AxisListType.X, op=ALU.max, negate=True
                )
            row_tiles.append({"s_ji": s_ji, "neg_max": neg_max})

        def exponentials(rt):
            t = row_tiles[rt]
            e_ji = t["e_ji"] = soft.tile([P, TOKENS, TOKENS], F32, name="e_ji")
            sums = t["sums"] = soft.tile([P, TOKENS], F32, name="sums")
            for j in range(J_BANK):
                nc.scalar.activation(
                    out=e_ji[:, j, :],
                    in_=t["s_ji"][:, j, :],
                    func=EXP,
                    bias=t["neg_max"][:, j : j + 1],
                    scale=1.0,
                    accum_out=sums[:, j : j + 1],
                )
            for j in range(J_BANK, TOKENS):
                nc.scalar.activation(
                    out=e_ji[:, j, :], in_=t["s_ji"][:, j, :], func=EXP, bias=t["neg_max"][:, j : j + 1], scale=1.0
                )
            js = slice(J_BANK, TOKENS)
            nc.vector.tensor_reduce(out=sums[:, js], in_=e_ji[:, js, :], axis=mybir.AxisListType.X, op=ALU.add)

        def normalise(rt):
            t = row_tiles[rt]
            inv = soft.tile([P, TOKENS], F32)
            o_ij = soft.tile([P, TOKENS, TOKENS], F32)
            engine = nc.vector if rt // ROW_TILES == GROUPS - 1 else nc.gpsimd
            o_blocks = o_ij[:].rearrange("p i (b q) -> p b i q", q=4)
            e_blocks = t["e_ji"][:].rearrange("p (b q) i -> p b i q", q=4)
            inv_blocks = inv[:].rearrange("p (b q) -> p b q", q=4).unsqueeze(2).to_broadcast([P, TOKENS // 4, TOKENS, 4])
            for b in range(BANKS):
                js = slice(b * J_BANK, (b + 1) * J_BANK)
                nc.vector.reciprocal(out=inv[:, js], in_=t["sums"][:, js])
                half = slice(b * J_BANK // 4, (b + 1) * J_BANK // 4)
                engine.tensor_tensor(out=o_blocks[:, half], in0=e_blocks[:, half], in1=inv_blocks[:, half], op=ALU.mult)
            nc.sync.dma_start(out=out_rows[rt * P : (rt + 1) * P, :], in_=o_ij[:].rearrange("p i j -> p (i j)"))

        def front_half(k):
            channels_to_partitions(k)
            quantise_x(k)
            compress(k)
            if k % 2 == 1:
                flatten(k // 2)

        prepare_wc()
        channels_to_partitions(0)
        channels_to_partitions(1)
        spread_biases()
        for k in range(2):
            quantise_x(k)
            compress(k)
        flatten(0)
        prepare_wg()
        for k in range(2, 2 + AHEAD):
            front_half(k)
        for rt in range(ALL_ROW_TILES):
            logits(rt)
            exponentials(rt)
            normalise(rt)
            if rt + 2 + AHEAD < HALVES:
                front_half(rt + 2 + AHEAD)
